import numpy as np
import ml_dtypes


def mxq(x, axis, fmt="e4m3"):
    dtype, down = {"e4m3": (ml_dtypes.float8_e4m3fn, 7), "e5m2": (ml_dtypes.float8_e5m2, 14)}[fmt]
    v = np.moveaxis(np.asarray(x, np.float32).astype(ml_dtypes.bfloat16).astype(np.float64), axis, -1)
    blocks = v.reshape(v.shape[:-1] + (-1, 32))
    amax = np.abs(blocks).max(-1, keepdims=True)
    byte = np.maximum(np.where(amax > 0, np.frexp(amax)[1] - 1 + 127, 0) - down, 1)
    scale = np.exp2(byte - 127.0)
    codes = (blocks / scale).astype(np.float32).astype(dtype).astype(np.float64)
    return np.moveaxis((codes * scale).reshape(v.shape), -1, axis)


WIDE = False


def mx_kscale(k):
    if not WIDE:
        return np.ones(k)
    levels = np.array([10, -10, 5, -5, 0])
    a = np.random.permutation(np.resize(levels, k // 512 * 4)).reshape(k // 512, 4)
    idx = np.arange(k)
    return np.exp2(a[idx // 512, idx % 128 // 32])


BF16 = ml_dtypes.bfloat16


def bf(x):
    return np.asarray(x, np.float32).astype(BF16)


def f64(x):
    return np.asarray(x).astype(np.float64)


N, T, H, P0, P1, C0, NC, V0, V1 = 4, 1024, 1024, 512, 128, 20000, 2, 1024, 12288


def setup_inputs():
    s, t = mx_kscale(H), mx_kscale(P0)
    return {"x": bf(np.random.standard_normal((N, T, H)) * s),
            "tail_proj_0": bf(np.random.standard_normal((H, P0)) / np.sqrt(H) / s[:, None] * t),
            "tail_w_0": bf(np.random.standard_normal((P0, V0)) * 2.0 / np.sqrt(P0) / t[:, None]),
            "cluster_prob": bf(0.05 + 0.55 * np.random.random((N, T))[..., None])}


def reference(x, tail_proj_0, tail_w_0, cluster_prob):
    h = mxq(f64(x), 2, "e4m3") @ mxq(f64(tail_proj_0), 0, "e4m3")
    logits = mxq(h, 2, "e4m3") @ mxq(f64(tail_w_0), 0, "e4m3")
    e = np.exp(logits - logits.max(-1, keepdims=True))
    return e / e.sum(-1, keepdims=True) * f64(cluster_prob)

@@ -1,0 +1,298 @@
+from contextlib import ExitStack
+
+import concourse.mybir as mybir
+from concourse.masks import make_identity
+
+F32 = mybir.dt.float32
+BF16 = mybir.dt.bfloat16
+U32 = mybir.dt.uint32
+U8 = mybir.dt.uint8
+FP8X4 = mybir.dt.float8_e4m3fn_x4
+ALU = mybir.AluOpType
+ACT = mybir.ActivationFunctionType
+AX = mybir.AxisListType
+
+P = 128
+TOKENS = 4096
+H = 1024
+P0 = 512
+V0 = 1024
+TILES = TOKENS // P
+PAIRS = TILES // 2
+
+FLOPS = 2 * TOKENS * H * P0 + 2 * TOKENS * P0 * V0
+
+MANUAL = True
+LH = 2
+LX = 3
+V_COPY_LO = 4
+V_COPY_HI = 32
+TAIL_PAIRS = 2
+GP_SCALE = True
+
+
+def tile_adaptiveinputsoftmax_pa_t_kernel(tc, x, tail_proj_0, tail_w_0, cluster_prob, out):
+    nc = tc.nc
+    with ExitStack() as ctx:
+        const = ctx.enter_context(tc.tile_pool(name="const", bufs=1))
+        xg_pool = ctx.enter_context(tc.tile_pool(name="xg_pool", bufs=3))
+        xc_pool = ctx.enter_context(tc.tile_pool(name="xc_pool", bufs=3))
+        hg_pool = ctx.enter_context(tc.tile_pool(name="hg_pool", bufs=2))
+        hc_pool = ctx.enter_context(tc.tile_pool(name="hc_pool", bufs=LH + 1))
+        e_pool = ctx.enter_context(tc.tile_pool(name="e_pool", bufs=4))
+        st_pool = ctx.enter_context(tc.tile_pool(name="st_pool", bufs=4))
+        pt_pool = ctx.enter_context(tc.psum_pool(name="pt_pool", bufs=2))
+        ph_pool = ctx.enter_context(tc.psum_pool(name="ph_pool", bufs=2))
+        pl_pool = ctx.enter_context(tc.psum_pool(name="pl_pool", bufs=4))
+        if MANUAL:
+            ctx.enter_context(tc.manual_schedule())
+
+        x_rows = x.flatten_outer_dims().rearrange("(p i) k -> p (i k)", i=TILES)
+        out_rows = out.flatten_outer_dims().rearrange("(p i) v -> p (i v)", i=TILES)
+        prob_rows = cluster_prob.rearrange("n t o -> (n t o)").rearrange("(p i) -> p i", i=TILES)
+
+        ident = const.tile([P, P], F32, name="ident")
+        make_identity(nc, ident[:])
+        warm_in = const.tile([P, 1], F32, name="warm_in")
+        warm_out = const.tile([P, 1], F32, name="warm_out")
+        nc.vector.memset(warm_in[:], 0.0)
+        nc.scalar.activation(out=warm_out[:], in_=warm_in[:], func=ACT.Exp)
+
+        p_raw = const.tile([P, 4096], BF16, name="p_raw")
+        p_grp = const.tile([P, 4096], BF16, name="p_grp", align_bytes=64)
+        p_cod = const.tile([P, 1024], U32, name="p_cod", align_bytes=64)
+        p_scl = const.tile([P, 1024], U8, name="p_scl", align_bytes=64)
+        w_raw = const.tile([P, 4096], BF16, name="w_raw")
+        w_grp = const.tile([P, 4096], BF16, name="w_grp", align_bytes=64)
+        w_cod = const.tile([P, 1024], U32, name="w_cod", align_bytes=64)
+        w_scl = const.tile([P, 1024], U8, name="w_scl", align_bytes=64)
+        prob_bf = const.tile([P, TILES], BF16, name="prob_bf")
+        prob = const.tile([P, TILES], F32, name="prob")
+        x_sb = [const.tile([P, 4096], BF16, name="x_sb%d" % g) for g in range(8)]
+
+        for c in range(2):
+            nc.sync.dma_start(
+                out=p_raw[:, 2048 * c : 2048 * (c + 1)].rearrange("p (u m) -> p u m", u=2),
+                in_=tail_proj_0[512 * c : 512 * (c + 1), :].rearrange("(u p e) n -> p u (e n)", u=2, e=2),
+            )
+        for a in range(2):
+            nc.sync.dma_start(out=x_sb[0][:, 2048 * a : 2048 * (a + 1)], in_=x_rows[:, 2048 * a : 2048 * (a + 1)])
+        nc.sync.dma_start(
+            out=w_raw[:].rearrange("p (t n) -> p t n", t=4),
+            in_=tail_w_0.rearrange("(t p) n -> p t n", t=4),
+        )
+        nc.sync.dma_start(out=prob_bf[:], in_=prob_rows)
+        for g in range(1, 8):
+            nc.sync.dma_start(out=x_sb[g][:], in_=x_rows[:, 4096 * g : 4096 * (g + 1)])
+
+        def prepare_proj():
+            for c in range(2):
+                cols = slice(2048 * c, 2048 * (c + 1))
+                nc.vector.tensor_copy(
+                    out=p_grp[:, cols].rearrange("p (a i t) -> p a t i", i=4, t=4),
+                    in_=p_raw[:, cols].rearrange("p (t a i) -> p a t i", t=4, i=4),
+                )
+            for c in range(2):
+                nc.vector.quantize_mx(
+                    out=p_cod[:, 512 * c : 512 * (c + 1)].bitcast(FP8X4),
+                    scales=p_scl[:, 512 * c : 512 * (c + 1)],
+                    in_=p_grp[:, 2048 * c : 2048 * (c + 1)],
+                )
+
+        def prepare_w():
+            planes = w_raw[:].rearrange("p (t n) -> p t n", t=4)
+            for v in range(2):
+                nc.vector.tensor_copy(
+                    out=w_grp[:, 2048 * v : 2048 * (v + 1)].rearrange("p (a i t) -> p a t i", i=4, t=4),
+                    in_=planes[:, :, 512 * v : 512 * (v + 1)].rearrange("p t (a i) -> p a t i", i=4),
+                )
+            for v in range(2):
+                nc.vector.quantize_mx(
+                    out=w_cod[:, 512 * v : 512 * (v + 1)].bitcast(FP8X4),
+                    scales=w_scl[:, 512 * v : 512 * (v + 1)],
+                    in_=w_grp[:, 2048 * v : 2048 * (v + 1)],
+                )
+            nc.vector.tensor_copy(out=prob[:], in_=prob_bf[:])
+
+        xt_of = {}
+        xg_of = {}
+        xc_of = {}
+        ht_of = {}
+        hg_of = {}
+        hc_of = {}
+        lg_of = {}
+        mx_of = {}
+        e_of = {}
+        sm_of = {}
+        rc_of = {}
+
+        def copy_engine(kind, i):
+            if kind == "x" and i % 2 == 1 and V_COPY_LO <= i < V_COPY_HI:
+                return nc.vector.tensor_copy
+            return nc.scalar.copy
+
+        def transposes(i):
+            words = x_sb[i // 4][:].bitcast(F32)
+            xt = pt_pool.tile([P, 4, P], F32, name="xt")
+            for s in range(4):
+                first = 512 * (i % 4) + P * s
+                nc.tensor.transpose(xt[:, s, :], words[:, first : first + P], ident[:])
+            xt_of[i] = xt
+
+        def copy_x(i):
+            q, a = divmod(i, 2)
+            if a == 0:
+                xg = xg_pool.tile([P, 2048], BF16, name="xg", align_bytes=64)
+                xg_of[q] = xg
+            copy_engine("x", i)(
+                out=xg_of[q][:, 1024 * a : 1024 * (a + 1)].bitcast(F32).rearrange("p (c r u) -> p c r u", c=2, u=2),
+                in_=xt_of[i][:].rearrange("p (c u) r -> p c r u", c=2),
+            )
+
+        def quantise_x(q):
+            cod = xc_pool.tile([P, 512], U32, name="x_cod", align_bytes=64)
+            scl = xc_pool.tile([P, 512], U8, name="x_scl", align_bytes=64)
+            nc.vector.quantize_mx(out=cod[:].bitcast(FP8X4), scales=scl[:], in_=xg_of[q][:])
+            xc_of[q] = (cod, scl)
+
+        def stage1(i, chunks):
+            q, a = divmod(i, 2)
+            cod, scl = xc_of[q]
+            if i not in ht_of:
+                ht = ph_pool.tile([P, 4, P], F32, name="ht")
+                ht_of[i] = ht
+            for t in chunks:
+                for c in range(2):
+                    wcols = slice(512 * c + P * t, 512 * c + P * (t + 1))
+                    xcols = slice(256 * a + P * c, 256 * a + P * (c + 1))
+                    nc.tensor.matmul_mx(
+                        out=ht_of[i][:, t, :],
+                        lhsT=p_cod[:, wcols].bitcast(FP8X4),
+                        lhsT_scale=p_scl[:, wcols],
+                        rhs=cod[:, xcols].bitcast(FP8X4),
+                        rhs_scale=scl[:, xcols],
+                        start=(c == 0),
+                        stop=(c == 1),
+                    )
+
+        def copy_h(i):
+            q, a = divmod(i, 2)
+            if a == 0:
+                hg = hg_pool.tile([P, 1024], BF16, name="hg", align_bytes=64)
+                hg_of[q] = hg
+            copy_engine("h", i)(
+                out=hg_of[q][:, 512 * a : 512 * (a + 1)].rearrange("p (r t) -> p r t", t=4),
+                in_=ht_of[i][:].rearrange("p t r -> p r t"),
+            )
+
+        def quantise_h(q):
+            cod = hc_pool.tile([P, 256], U32, name="h_cod", align_bytes=64)
+            scl = hc_pool.tile([P, 256], U8, name="h_scl", align_bytes=64)
+            nc.vector.quantize_mx(out=cod[:].bitcast(FP8X4), scales=scl[:], in_=hg_of[q][:])
+            hc_of[q] = (cod, scl)
+
+        def stage2(i, v):
+            q, a = divmod(i, 2)
+            cod, scl = hc_of[q]
+            lg = pl_pool.tile([P, 512], F32, name="lg")
+            nc.tensor.matmul_mx(
+                out=lg[:],
+                lhsT=cod[:, P * a : P * (a + 1)].bitcast(FP8X4),
+                lhsT_scale=scl[:, P * a : P * (a + 1)],
+                rhs=w_cod[:, 512 * v : 512 * (v + 1)].bitcast(FP8X4),
+                rhs_scale=w_scl[:, 512 * v : 512 * (v + 1)],
+                start=True,
+                stop=True,
+            )
+            lg_of[(i, v)] = lg
+
+        def row_max(i, v):
+            if v == 0:
+                mx = st_pool.tile([P, 4], F32, name="mx")
+                mx_of[i] = mx
+            mx = mx_of[i]
+            nc.vector.tensor_reduce(out=mx[:, v : v + 1], in_=lg_of[(i, v)][:], axis=AX.X, op=ALU.max)
+            if v == 1:
+                nc.vector.tensor_scalar(
+                    out=mx[:, 2:3], in0=mx[:, 0:1], scalar1=mx[:, 1:2], scalar2=-1.0, op0=ALU.max, op1=ALU.mult
+                )
+
+        def exponent(i, v):
+            q, a = divmod(i, 2)
+            if a == 0 and v == 0:
+                e = e_pool.tile([P, 2048], F32, name="e")
+                sm = st_pool.tile([P, 4], F32, name="sm")
+                rc = st_pool.tile([P, 4], F32, name="rc")
+                e_of[q] = e
+                sm_of[q] = sm
+                rc_of[q] = rc
+            first = 1024 * a + 512 * v
+            nc.scalar.activation(
+                out=e_of[q][:, first : first + 512],
+                in_=lg_of[(i, v)][:],
+                func=ACT.Exp,
+                bias=mx_of[i][:, 2:3],
+                scale=1.0,
+                accum_out=sm_of[q][:, 2 * a + v : 2 * a + v + 1],
+            )
+
+        def finish(q, halves, engine):
+            lo, n = halves[0], len(halves)
+            sm = sm_of[q]
+            rc = rc_of[q]
+            nc.vector.tensor_reduce(
+                out=rc[:, lo : lo + n],
+                in_=sm[:, 2 * lo : 2 * (lo + n)].rearrange("p (a v) -> p a v", v=2),
+                axis=AX.X,
+                op=ALU.add,
+            )
+            nc.vector.reciprocal(out=rc[:, 2 + lo : 2 + lo + n], in_=rc[:, lo : lo + n])
+            for a in halves:
+                i = 2 * q + a
+                part = e_of[q][:, 1024 * a : 1024 * (a + 1)]
+                engine.tensor_scalar(
+                    out=part,
+                    in0=part,
+                    scalar1=rc[:, 2 + a : 3 + a],
+                    scalar2=prob[:, i : i + 1],
+                    op0=ALU.mult,
+                    op1=ALU.mult,
+                )
+            nc.sync.dma_start(
+                out=out_rows[:, 2048 * q + 1024 * lo : 2048 * q + 1024 * (lo + n)],
+                in_=e_of[q][:, 1024 * lo : 1024 * (lo + n)],
+            )
+
+        def live(q):
+            return 0 <= q < PAIRS
+
+        prepare_proj()
+        for q in range(-LX, PAIRS + 1):
+            if q == -2:
+                prepare_w()
+            if live(q + LX):
+                transposes(2 * (q + LX))
+                transposes(2 * (q + LX) + 1)
+            if live(q - 1) and q - 1 < PAIRS - TAIL_PAIRS:
+                finish(q - 1, [0, 1], nc.gpsimd if GP_SCALE else nc.vector)
+            for b in range(4):
+                a, v = divmod(b, 2)
+                if live(q):
+                    exponent(2 * q + a, v)
+                if live(q + 1):
+                    stage2(2 * (q + 1) + a, v)
+                if live(q + LH):
+                    stage1(2 * (q + LH) + a, [2 * v, 2 * v + 1])
+                if live(q + 1):
+                    row_max(2 * (q + 1) + a, v)
+                if live(q) and q >= PAIRS - TAIL_PAIRS and v == 1:
+                    finish(q, [a], nc.vector)
+            for a in range(2):
+                if live(q + LH):
+                    copy_h(2 * (q + LH) + a)
+                if live(q + LX):
+                    copy_x(2 * (q + LX) + a)
+            if live(q + LH):
+                quantise_h(q + LH)
+            if live(q + LH + 1):
+                quantise_x(q + LH + 1)

@@ -22,7 +22,7 @@ PAIRS = TILES // 2
 
 FLOPS = 2 * TOKENS * H * P0 + 2 * TOKENS * P0 * V0
 
-MANUAL = True
+MANUAL = False
 LH = 2
 LX = 3
 V_COPY_LO = 4

@@ -213,9 +213,7 @@ def tile_adaptiveinputsoftmax_pa_t_kernel(tc, x, tail_proj_0, tail_w_0, cluster_
             mx = mx_of[i]
             nc.vector.tensor_reduce(out=mx[:, v : v + 1], in_=lg_of[(i, v)][:], axis=AX.X, op=ALU.max)
             if v == 1:
-                nc.vector.tensor_scalar(
-                    out=mx[:, 2:3], in0=mx[:, 0:1], scalar1=mx[:, 1:2], scalar2=-1.0, op0=ALU.max, op1=ALU.mult
-                )
+                nc.vector.tensor_reduce(out=mx[:, 2:3], in_=mx[:, 0:2], axis=AX.X, op=ALU.max, negate=True)
 
         def exponent(i, v):
             q, a = divmod(i, 2)

@@ -23,27 +23,25 @@ PAIRS = TILES // 2
 FLOPS = 2 * TOKENS * H * P0 + 2 * TOKENS * P0 * V0
 
 MANUAL = False
-LH = 2
-LX = 3
-V_COPY_LO = 4
-V_COPY_HI = 32
-TAIL_PAIRS = 2
-GP_SCALE = True
+QUADS = 8
+S_XC = 3
+S_HC = 3
+DELAY = 2
+TAIL = 6
+EARLY = 2
+GTAIL = 0
 
 
 def tile_adaptiveinputsoftmax_pa_t_kernel(tc, x, tail_proj_0, tail_w_0, cluster_prob, out):
     nc = tc.nc
     with ExitStack() as ctx:
         const = ctx.enter_context(tc.tile_pool(name="const", bufs=1))
-        xg_pool = ctx.enter_context(tc.tile_pool(name="xg_pool", bufs=3))
-        xc_pool = ctx.enter_context(tc.tile_pool(name="xc_pool", bufs=3))
+        xg_pool = ctx.enter_context(tc.tile_pool(name="xg_pool", bufs=2))
+        xc_pool = ctx.enter_context(tc.tile_pool(name="xc_pool", bufs=2))
         hg_pool = ctx.enter_context(tc.tile_pool(name="hg_pool", bufs=2))
-        hc_pool = ctx.enter_context(tc.tile_pool(name="hc_pool", bufs=LH + 1))
-        e_pool = ctx.enter_context(tc.tile_pool(name="e_pool", bufs=4))
-        st_pool = ctx.enter_context(tc.tile_pool(name="st_pool", bufs=4))
-        pt_pool = ctx.enter_context(tc.psum_pool(name="pt_pool", bufs=2))
-        ph_pool = ctx.enter_context(tc.psum_pool(name="ph_pool", bufs=2))
-        pl_pool = ctx.enter_context(tc.psum_pool(name="pl_pool", bufs=4))
+        e_pool = ctx.enter_context(tc.tile_pool(name="e_pool", bufs=5))
+        st_pool = ctx.enter_context(tc.tile_pool(name="st_pool", bufs=8))
+        ps_pool = ctx.enter_context(tc.psum_pool(name="ps_pool", bufs=8))
         if MANUAL:
             ctx.enter_context(tc.manual_schedule())
 
@@ -68,6 +66,8 @@ def tile_adaptiveinputsoftmax_pa_t_kernel(tc, x, tail_proj_0, tail_w_0, cluster_
         w_scl = const.tile([P, 1024], U8, name="w_scl", align_bytes=64)
         prob_bf = const.tile([P, TILES], BF16, name="prob_bf")
         prob = const.tile([P, TILES], F32, name="prob")
+        h_cod = const.tile([P, TOKENS], U32, name="h_cod", align_bytes=64)
+        h_scl = const.tile([P, TOKENS], U8, name="h_scl", align_bytes=64)
         x_sb = [const.tile([P, 4096], BF16, name="x_sb%d" % g) for g in range(8)]
 
         for c in range(2):
@@ -77,13 +77,14 @@ def tile_adaptiveinputsoftmax_pa_t_kernel(tc, x, tail_proj_0, tail_w_0, cluster_
             )
         for a in range(2):
             nc.sync.dma_start(out=x_sb[0][:, 2048 * a : 2048 * (a + 1)], in_=x_rows[:, 2048 * a : 2048 * (a + 1)])
-        nc.sync.dma_start(
-            out=w_raw[:].rearrange("p (t n) -> p t n", t=4),
-            in_=tail_w_0.rearrange("(t p) n -> p t n", t=4),
-        )
-        nc.sync.dma_start(out=prob_bf[:], in_=prob_rows)
         for g in range(1, 8):
             nc.sync.dma_start(out=x_sb[g][:], in_=x_rows[:, 4096 * g : 4096 * (g + 1)])
+            if g == 1:
+                nc.sync.dma_start(
+                    out=w_raw[:].rearrange("p (t n) -> p t n", t=4),
+                    in_=tail_w_0.rearrange("(t p) n -> p t n", t=4),
+                )
+                nc.sync.dma_start(out=prob_bf[:], in_=prob_rows)
 
         def prepare_proj():
             for c in range(2):
@@ -119,120 +120,115 @@ def tile_adaptiveinputsoftmax_pa_t_kernel(tc, x, tail_proj_0, tail_w_0, cluster_
         xc_of = {}
         ht_of = {}
         hg_of = {}
-        hc_of = {}
         lg_of = {}
         mx_of = {}
         e_of = {}
         sm_of = {}
         rc_of = {}
 
-        def copy_engine(kind, i):
-            if kind == "x" and i % 2 == 1 and V_COPY_LO <= i < V_COPY_HI:
-                return nc.vector.tensor_copy
-            return nc.scalar.copy
+        def transposes(g):
+            words = x_sb[g][:].bitcast(F32)
+            for j in range(4):
+                xt = ps_pool.tile([P, 512], F32, name="bank")
+                for s in range(4):
+                    first = 512 * j + P * s
+                    nc.tensor.transpose(xt[:, P * s : P * (s + 1)], words[:, first : first + P], ident[:])
+                xt_of[4 * g + j] = xt
 
-        def transposes(i):
-            words = x_sb[i // 4][:].bitcast(F32)
-            xt = pt_pool.tile([P, 4, P], F32, name="xt")
-            for s in range(4):
-                first = 512 * (i % 4) + P * s
-                nc.tensor.transpose(xt[:, s, :], words[:, first : first + P], ident[:])
-            xt_of[i] = xt
+        def copy_x(g):
+            xg = xg_pool.tile([P, 4096], BF16, name="xg", align_bytes=64)
+            xg_of[g] = xg
+            for j in range(4):
+                copy = nc.scalar.copy if j < S_XC else nc.vector.tensor_copy
+                copy(
+                    out=xg[:, 1024 * j : 1024 * (j + 1)].bitcast(F32).rearrange("p (c r u) -> p c r u", c=2, u=2),
+                    in_=xt_of[4 * g + j][:].rearrange("p (c u r) -> p c r u", c=2, u=2),
+                )
 
-        def copy_x(i):
+        def quantise_x(g):
+            cod = xc_pool.tile([P, 1024], U32, name="x_cod", align_bytes=64)
+            scl = xc_pool.tile([P, 1024], U8, name="x_scl", align_bytes=64)
+            for a in range(2):
+                nc.vector.quantize_mx(
+                    out=cod[:, 512 * a : 512 * (a + 1)].bitcast(FP8X4),
+                    scales=scl[:, 512 * a : 512 * (a + 1)],
+                    in_=xg_of[g][:, 2048 * a : 2048 * (a + 1)],
+                )
+            xc_of[g] = (cod, scl)
+
+        def stage1(g):
+            cod, scl = xc_of[g]
+            for j in range(4):
+                ht = ps_pool.tile([P, 512], F32, name="bank")
+                ht_of[4 * g + j] = ht
+                for t in range(4):
+                    for c in range(2):
+                        wcols = slice(512 * c + P * t, 512 * c + P * (t + 1))
+                        xcols = slice(256 * j + P * c, 256 * j + P * (c + 1))
+                        nc.tensor.matmul_mx(
+                            out=ht[:, P * t : P * (t + 1)],
+                            lhsT=p_cod[:, wcols].bitcast(FP8X4),
+                            lhsT_scale=p_scl[:, wcols],
+                            rhs=cod[:, xcols].bitcast(FP8X4),
+                            rhs_scale=scl[:, xcols],
+                            start=(c == 0),
+                            stop=(c == 1),
+                        )
+
+        def copy_h(g):
+            hg = hg_pool.tile([P, 2048], BF16, name="hg", align_bytes=64)
+            hg_of[g] = hg
+            for j in range(4):
+                copy = nc.scalar.copy if (j < S_HC or g == QUADS - 1) else nc.vector.tensor_copy
+                copy(
+                    out=hg[:, 512 * j : 512 * (j + 1)].rearrange("p (r t) -> p r t", t=4),
+                    in_=ht_of[4 * g + j][:].rearrange("p (t r) -> p r t", t=4),
+                )
+
+        def quantise_h(g):
+            cols = slice(512 * g, 512 * (g + 1))
+            nc.vector.quantize_mx(out=h_cod[:, cols].bitcast(FP8X4), scales=h_scl[:, cols], in_=hg_of[g][:])
+
+        def stage2(i):
+            for v in range(2):
+                lg = ps_pool.tile([P, 512], F32, name="bank")
+                nc.tensor.matmul_mx(
+                    out=lg[:],
+                    lhsT=h_cod[:, P * i : P * (i + 1)].bitcast(FP8X4),
+                    lhsT_scale=h_scl[:, P * i : P * (i + 1)],
+                    rhs=w_cod[:, 512 * v : 512 * (v + 1)].bitcast(FP8X4),
+                    rhs_scale=w_scl[:, 512 * v : 512 * (v + 1)],
+                    start=True,
+                    stop=True,
+                )
+                lg_of[(i, v)] = lg
+
+        def row_max(i):
+            mx = st_pool.tile([P, 4], F32, name="mx")
+            mx_of[i] = mx
+            for v in range(2):
+                nc.vector.tensor_reduce(out=mx[:, v : v + 1], in_=lg_of[(i, v)][:], axis=AX.X, op=ALU.max)
+            nc.vector.tensor_reduce(out=mx[:, 2:3], in_=mx[:, 0:2], axis=AX.X, op=ALU.max, negate=True)
+
+        def exponent(i):
             q, a = divmod(i, 2)
             if a == 0:
-                xg = xg_pool.tile([P, 2048], BF16, name="xg", align_bytes=64)
-                xg_of[q] = xg
-            copy_engine("x", i)(
-                out=xg_of[q][:, 1024 * a : 1024 * (a + 1)].bitcast(F32).rearrange("p (c r u) -> p c r u", c=2, u=2),
-                in_=xt_of[i][:].rearrange("p (c u) r -> p c r u", c=2),
-            )
-
-        def quantise_x(q):
-            cod = xc_pool.tile([P, 512], U32, name="x_cod", align_bytes=64)
-            scl = xc_pool.tile([P, 512], U8, name="x_scl", align_bytes=64)
-            nc.vector.quantize_mx(out=cod[:].bitcast(FP8X4), scales=scl[:], in_=xg_of[q][:])
-            xc_of[q] = (cod, scl)
-
-        def stage1(i, chunks):
-            q, a = divmod(i, 2)
-            cod, scl = xc_of[q]
-            if i not in ht_of:
-                ht = ph_pool.tile([P, 4, P], F32, name="ht")
-                ht_of[i] = ht
-            for t in chunks:
-                for c in range(2):
-                    wcols = slice(512 * c + P * t, 512 * c + P * (t + 1))
-                    xcols = slice(256 * a + P * c, 256 * a + P * (c + 1))
-                    nc.tensor.matmul_mx(
-                        out=ht_of[i][:, t, :],
-                        lhsT=p_cod[:, wcols].bitcast(FP8X4),
-                        lhsT_scale=p_scl[:, wcols],
-                        rhs=cod[:, xcols].bitcast(FP8X4),
-                        rhs_scale=scl[:, xcols],
-                        start=(c == 0),
-                        stop=(c == 1),
-                    )
-
-        def copy_h(i):
-            q, a = divmod(i, 2)
-            if a == 0:
-                hg = hg_pool.tile([P, 1024], BF16, name="hg", align_bytes=64)
-                hg_of[q] = hg
-            copy_engine("h", i)(
-                out=hg_of[q][:, 512 * a : 512 * (a + 1)].rearrange("p (r t) -> p r t", t=4),
-                in_=ht_of[i][:].rearrange("p t r -> p r t"),
-            )
-
-        def quantise_h(q):
-            cod = hc_pool.tile([P, 256], U32, name="h_cod", align_bytes=64)
-            scl = hc_pool.tile([P, 256], U8, name="h_scl", align_bytes=64)
-            nc.vector.quantize_mx(out=cod[:].bitcast(FP8X4), scales=scl[:], in_=hg_of[q][:])
-            hc_of[q] = (cod, scl)
-
-        def stage2(i, v):
-            q, a = divmod(i, 2)
-            cod, scl = hc_of[q]
-            lg = pl_pool.tile([P, 512], F32, name="lg")
-            nc.tensor.matmul_mx(
-                out=lg[:],
-                lhsT=cod[:, P * a : P * (a + 1)].bitcast(FP8X4),
-                lhsT_scale=scl[:, P * a : P * (a + 1)],
-                rhs=w_cod[:, 512 * v : 512 * (v + 1)].bitcast(FP8X4),
-                rhs_scale=w_scl[:, 512 * v : 512 * (v + 1)],
-                start=True,
-                stop=True,
-            )
-            lg_of[(i, v)] = lg
-
-        def row_max(i, v):
-            if v == 0:
-                mx = st_pool.tile([P, 4], F32, name="mx")
-                mx_of[i] = mx
-            mx = mx_of[i]
-            nc.vector.tensor_reduce(out=mx[:, v : v + 1], in_=lg_of[(i, v)][:], axis=AX.X, op=ALU.max)
-            if v == 1:
-                nc.vector.tensor_reduce(out=mx[:, 2:3], in_=mx[:, 0:2], axis=AX.X, op=ALU.max, negate=True)
-
-        def exponent(i, v):
-            q, a = divmod(i, 2)
-            if a == 0 and v == 0:
                 e = e_pool.tile([P, 2048], F32, name="e")
                 sm = st_pool.tile([P, 4], F32, name="sm")
                 rc = st_pool.tile([P, 4], F32, name="rc")
                 e_of[q] = e
                 sm_of[q] = sm
                 rc_of[q] = rc
-            first = 1024 * a + 512 * v
-            nc.scalar.activation(
-                out=e_of[q][:, first : first + 512],
-                in_=lg_of[(i, v)][:],
-                func=ACT.Exp,
-                bias=mx_of[i][:, 2:3],
-                scale=1.0,
-                accum_out=sm_of[q][:, 2 * a + v : 2 * a + v + 1],
-            )
+            for v in range(2):
+                first = 1024 * a + 512 * v
+                nc.scalar.activation(
+                    out=e_of[q][:, first : first + 512],
+                    in_=lg_of[(i, v)][:],
+                    func=ACT.Exp,
+                    bias=mx_of[i][:, 2:3],
+                    scale=1.0,
+                    accum_out=sm_of[q][:, 2 * a + v : 2 * a + v + 1],
+                )
 
         def finish(q, halves, engine):
             lo, n = halves[0], len(halves)
@@ -256,41 +252,42 @@ def tile_adaptiveinputsoftmax_pa_t_kernel(tc, x, tail_proj_0, tail_w_0, cluster_
                     op0=ALU.mult,
                     op1=ALU.mult,
                 )
-            nc.sync.dma_start(
-                out=out_rows[:, 2048 * q + 1024 * lo : 2048 * q + 1024 * (lo + n)],
-                in_=e_of[q][:, 1024 * lo : 1024 * (lo + n)],
-            )
+                nc.sync.dma_start(out=out_rows[:, 1024 * i : 1024 * (i + 1)], in_=part)
 
-        def live(q):
-            return 0 <= q < PAIRS
+        def back_end(i):
+            if i < TILES:
+                stage2(i)
+                row_max(i)
+                exponent(i)
+            if i == EARLY + 1:
+                quantise_h(QUADS - 1)
+            d = i - DELAY
+            if d >= 0 and d % 2 == 1 and d < TILES - TAIL:
+                finish(d // 2, [0, 1], nc.gpsimd)
+            if d == TILES - TAIL and d % 2 == 0 and GTAIL:
+                finish(d // 2, [0], nc.gpsimd)
 
         prepare_proj()
-        for q in range(-LX, PAIRS + 1):
-            if q == -2:
+        transposes(0)
+        copy_x(0)
+        quantise_x(0)
+        for g in range(QUADS):
+            if g + 1 < QUADS:
+                transposes(g + 1)
+            else:
+                for i in range(EARLY):
+                    back_end(i)
+            stage1(g)
+            if g + 1 < QUADS:
+                copy_x(g + 1)
+                quantise_x(g + 1)
+            if g == 1:
                 prepare_w()
-            if live(q + LX):
-                transposes(2 * (q + LX))
-                transposes(2 * (q + LX) + 1)
-            if live(q - 1) and q - 1 < PAIRS - TAIL_PAIRS:
-                finish(q - 1, [0, 1], nc.gpsimd if GP_SCALE else nc.vector)
-            for b in range(4):
-                a, v = divmod(b, 2)
-                if live(q):
-                    exponent(2 * q + a, v)
-                if live(q + 1):
-                    stage2(2 * (q + 1) + a, v)
-                if live(q + LH):
-                    stage1(2 * (q + LH) + a, [2 * v, 2 * v + 1])
-                if live(q + 1):
-                    row_max(2 * (q + 1) + a, v)
-                if live(q) and q >= PAIRS - TAIL_PAIRS and v == 1:
-                    finish(q, [a], nc.vector)
-            for a in range(2):
-                if live(q + LH):
-                    copy_h(2 * (q + LH) + a)
-                if live(q + LX):
-                    copy_x(2 * (q + LX) + a)
-            if live(q + LH):
-                quantise_h(q + LH)
-            if live(q + LH + 1):
-                quantise_x(q + LH + 1)
+            copy_h(g)
+            if g + 1 < QUADS:
+                quantise_h(g)
+        for i in range(EARLY, TILES + DELAY):
+            back_end(i)
+            if i == TILES - 1:
+                for d in range(TILES - TAIL + GTAIL, TILES):
+                    finish(d // 2, [d % 2], nc.vector)

@@ -22,14 +22,17 @@ PAIRS = TILES // 2
 
 FLOPS = 2 * TOKENS * H * P0 + 2 * TOKENS * P0 * V0
 
-MANUAL = False
+MANUAL = 0
 QUADS = 8
-S_XC = 3
-S_HC = 3
+XC_V = 1
+HC_VMOD = 4
+B_FIRST = 2
+RB = 4
 DELAY = 2
 TAIL = 6
-EARLY = 2
-GTAIL = 0
+W_AFTER = 4
+W_STEP = 5
+XBUFS = 5
 
 
 def tile_adaptiveinputsoftmax_pa_t_kernel(tc, x, tail_proj_0, tail_w_0, cluster_prob, out):
@@ -37,11 +40,11 @@ def tile_adaptiveinputsoftmax_pa_t_kernel(tc, x, tail_proj_0, tail_w_0, cluster_
     with ExitStack() as ctx:
         const = ctx.enter_context(tc.tile_pool(name="const", bufs=1))
         xg_pool = ctx.enter_context(tc.tile_pool(name="xg_pool", bufs=2))
-        xc_pool = ctx.enter_context(tc.tile_pool(name="xc_pool", bufs=2))
-        hg_pool = ctx.enter_context(tc.tile_pool(name="hg_pool", bufs=2))
+        x_pool = ctx.enter_context(tc.tile_pool(name="x_pool", bufs=XBUFS))
+        hg_pool = ctx.enter_context(tc.tile_pool(name="hg_pool", bufs=3))
         e_pool = ctx.enter_context(tc.tile_pool(name="e_pool", bufs=5))
         st_pool = ctx.enter_context(tc.tile_pool(name="st_pool", bufs=8))
-        ps_pool = ctx.enter_context(tc.psum_pool(name="ps_pool", bufs=8))
+        ps_pool = ctx.enter_context(tc.psum_pool(name="ps_pool", bufs=1))
         if MANUAL:
             ctx.enter_context(tc.manual_schedule())
 
@@ -68,7 +71,12 @@ def tile_adaptiveinputsoftmax_pa_t_kernel(tc, x, tail_proj_0, tail_w_0, cluster_
         prob = const.tile([P, TILES], F32, name="prob")
         h_cod = const.tile([P, TOKENS], U32, name="h_cod", align_bytes=64)
         h_scl = const.tile([P, TOKENS], U8, name="h_scl", align_bytes=64)
-        x_sb = [const.tile([P, 4096], BF16, name="x_sb%d" % g) for g in range(8)]
+        x_cod = const.tile([P, 2 * TOKENS], U32, name="x_cod", align_bytes=64)
+        x_scl = const.tile([P, 2 * TOKENS], U8, name="x_scl", align_bytes=64)
+        x_sb = []
+        for g in range(8):
+            xs = x_pool.tile([P, 4096], BF16, name="xs")
+            x_sb.append(xs)
 
         for c in range(2):
             nc.sync.dma_start(
@@ -79,7 +87,7 @@ def tile_adaptiveinputsoftmax_pa_t_kernel(tc, x, tail_proj_0, tail_w_0, cluster_
             nc.sync.dma_start(out=x_sb[0][:, 2048 * a : 2048 * (a + 1)], in_=x_rows[:, 2048 * a : 2048 * (a + 1)])
         for g in range(1, 8):
             nc.sync.dma_start(out=x_sb[g][:], in_=x_rows[:, 4096 * g : 4096 * (g + 1)])
-            if g == 1:
+            if g == W_AFTER:
                 nc.sync.dma_start(
                     out=w_raw[:].rearrange("p (t n) -> p t n", t=4),
                     in_=tail_w_0.rearrange("(t p) n -> p t n", t=4),
@@ -117,7 +125,6 @@ def tile_adaptiveinputsoftmax_pa_t_kernel(tc, x, tail_proj_0, tail_w_0, cluster_
 
         xt_of = {}
         xg_of = {}
-        xc_of = {}
         ht_of = {}
         hg_of = {}
         lg_of = {}
@@ -126,10 +133,13 @@ def tile_adaptiveinputsoftmax_pa_t_kernel(tc, x, tail_proj_0, tail_w_0, cluster_
         sm_of = {}
         rc_of = {}
 
+        def bank(b, name):
+            return ps_pool.tile([P, 512], F32, name=name, offset=2048 * b)
+
         def transposes(g):
             words = x_sb[g][:].bitcast(F32)
             for j in range(4):
-                xt = ps_pool.tile([P, 512], F32, name="bank")
+                xt = bank(j, "xt")
                 for s in range(4):
                     first = 512 * j + P * s
                     nc.tensor.transpose(xt[:, P * s : P * (s + 1)], words[:, first : first + P], ident[:])
@@ -139,59 +149,53 @@ def tile_adaptiveinputsoftmax_pa_t_kernel(tc, x, tail_proj_0, tail_w_0, cluster_
             xg = xg_pool.tile([P, 4096], BF16, name="xg", align_bytes=64)
             xg_of[g] = xg
             for j in range(4):
-                copy = nc.scalar.copy if j < S_XC else nc.vector.tensor_copy
+                copy = nc.vector.tensor_copy if j >= 4 - XC_V else nc.scalar.copy
                 copy(
                     out=xg[:, 1024 * j : 1024 * (j + 1)].bitcast(F32).rearrange("p (c r u) -> p c r u", c=2, u=2),
                     in_=xt_of[4 * g + j][:].rearrange("p (c u r) -> p c r u", c=2, u=2),
                 )
 
         def quantise_x(g):
-            cod = xc_pool.tile([P, 1024], U32, name="x_cod", align_bytes=64)
-            scl = xc_pool.tile([P, 1024], U8, name="x_scl", align_bytes=64)
             for a in range(2):
+                cols = slice(1024 * g + 512 * a, 1024 * g + 512 * (a + 1))
                 nc.vector.quantize_mx(
-                    out=cod[:, 512 * a : 512 * (a + 1)].bitcast(FP8X4),
-                    scales=scl[:, 512 * a : 512 * (a + 1)],
-                    in_=xg_of[g][:, 2048 * a : 2048 * (a + 1)],
-                )
-            xc_of[g] = (cod, scl)
-
-        def stage1(g):
-            cod, scl = xc_of[g]
-            for j in range(4):
-                ht = ps_pool.tile([P, 512], F32, name="bank")
-                ht_of[4 * g + j] = ht
-                for t in range(4):
-                    for c in range(2):
-                        wcols = slice(512 * c + P * t, 512 * c + P * (t + 1))
-                        xcols = slice(256 * j + P * c, 256 * j + P * (c + 1))
-                        nc.tensor.matmul_mx(
-                            out=ht[:, P * t : P * (t + 1)],
-                            lhsT=p_cod[:, wcols].bitcast(FP8X4),
-                            lhsT_scale=p_scl[:, wcols],
-                            rhs=cod[:, xcols].bitcast(FP8X4),
-                            rhs_scale=scl[:, xcols],
-                            start=(c == 0),
-                            stop=(c == 1),
-                        )
-
-        def copy_h(g):
-            hg = hg_pool.tile([P, 2048], BF16, name="hg", align_bytes=64)
-            hg_of[g] = hg
-            for j in range(4):
-                copy = nc.scalar.copy if (j < S_HC or g == QUADS - 1) else nc.vector.tensor_copy
-                copy(
-                    out=hg[:, 512 * j : 512 * (j + 1)].rearrange("p (r t) -> p r t", t=4),
-                    in_=ht_of[4 * g + j][:].rearrange("p (t r) -> p r t", t=4),
+                    out=x_cod[:, cols].bitcast(FP8X4), scales=x_scl[:, cols], in_=xg_of[g][:, 2048 * a : 2048 * (a + 1)]
                 )
 
-        def quantise_h(g):
-            cols = slice(512 * g, 512 * (g + 1))
-            nc.vector.quantize_mx(out=h_cod[:, cols].bitcast(FP8X4), scales=h_scl[:, cols], in_=hg_of[g][:])
+        def stage1(i):
+            ht = bank(4 + i % 4, "ht")
+            ht_of[i] = ht
+            for t in range(4):
+                for c in range(2):
+                    wcols = slice(512 * c + P * t, 512 * c + P * (t + 1))
+                    xcols = slice(256 * i + P * c, 256 * i + P * (c + 1))
+                    nc.tensor.matmul_mx(
+                        out=ht[:, P * t : P * (t + 1)],
+                        lhsT=p_cod[:, wcols].bitcast(FP8X4),
+                        lhsT_scale=p_scl[:, wcols],
+                        rhs=x_cod[:, xcols].bitcast(FP8X4),
+                        rhs_scale=x_scl[:, xcols],
+                        start=(c == 0),
+                        stop=(c == 1),
+                    )
 
-        def stage2(i):
+        def copy_h(i):
+            q, a = divmod(i, 2)
+            if a == 0:
+                hg = hg_pool.tile([P, 1024], BF16, name="hg", align_bytes=64)
+                hg_of[q] = hg
+            copy = nc.vector.tensor_copy if i % HC_VMOD == HC_VMOD - 1 else nc.scalar.copy
+            copy(
+                out=hg_of[q][:, 512 * a : 512 * (a + 1)].rearrange("p (r t) -> p r t", t=4),
+                in_=ht_of[i][:].rearrange("p (t r) -> p r t", t=4),
+            )
+            if a == 1:
+                cols = slice(256 * q, 256 * (q + 1))
+                nc.vector.quantize_mx(out=h_cod[:, cols].bitcast(FP8X4), scales=h_scl[:, cols], in_=hg_of[q][:])
+
+        def stage2(i, banks):
             for v in range(2):
-                lg = ps_pool.tile([P, 512], F32, name="bank")
+                lg = bank(banks[v], "lg")
                 nc.tensor.matmul_mx(
                     out=lg[:],
                     lhsT=h_cod[:, P * i : P * (i + 1)].bitcast(FP8X4),
@@ -254,40 +258,48 @@ def tile_adaptiveinputsoftmax_pa_t_kernel(tc, x, tail_proj_0, tail_w_0, cluster_
                 )
                 nc.sync.dma_start(out=out_rows[:, 1024 * i : 1024 * (i + 1)], in_=part)
 
-        def back_end(i):
-            if i < TILES:
-                stage2(i)
-                row_max(i)
-                exponent(i)
-            if i == EARLY + 1:
-                quantise_h(QUADS - 1)
+        state = {"b": 0, "c": 0}
+
+        def front_tile():
+            i = state["b"]
+            stage1(i)
+            copy_h(i)
+            state["b"] = i + 1
+
+        def soft_tile(banks):
+            i = state["c"]
+            stage2(i, banks)
+            row_max(i)
+            exponent(i)
+            state["c"] = i + 1
             d = i - DELAY
             if d >= 0 and d % 2 == 1 and d < TILES - TAIL:
                 finish(d // 2, [0, 1], nc.gpsimd)
-            if d == TILES - TAIL and d % 2 == 0 and GTAIL:
-                finish(d // 2, [0], nc.gpsimd)
 
         prepare_proj()
-        transposes(0)
-        copy_x(0)
-        quantise_x(0)
         for g in range(QUADS):
-            if g + 1 < QUADS:
-                transposes(g + 1)
-            else:
-                for i in range(EARLY):
-                    back_end(i)
-            stage1(g)
-            if g + 1 < QUADS:
-                copy_x(g + 1)
-                quantise_x(g + 1)
-            if g == 1:
+            transposes(g)
+            copy_x(g)
+            if g >= B_FIRST:
+                front_tile()
+            quantise_x(g)
+            if g == W_STEP:
                 prepare_w()
-            copy_h(g)
-            if g + 1 < QUADS:
-                quantise_h(g)
-        for i in range(EARLY, TILES + DELAY):
-            back_end(i)
-            if i == TILES - 1:
-                for d in range(TILES - TAIL + GTAIL, TILES):
-                    finish(d // 2, [d % 2], nc.vector)
+        while state["b"] < TILES:
+            for k in range(RB):
+                if state["b"] < TILES:
+                    front_tile()
+            c = state["c"]
+            soft_tile([(2 * c) % 4, (2 * c + 1) % 4])
+        if state["c"] % 2 == 1:
+            c = state["c"]
+            soft_tile([(2 * c) % 4, (2 * c + 1) % 4])
+        c0 = state["c"]
+        while state["c"] < TILES:
+            c = state["c"]
+            soft_tile([(2 * (c - c0) + 4) % 8, (2 * (c - c0) + 5) % 8])
+        for d in range(TILES - DELAY, TILES):
+            if d % 2 == 1 and d < TILES - TAIL:
+                finish(d // 2, [0, 1], nc.gpsimd)
+        for d in range(TILES - TAIL, TILES):
+            finish(d // 2, [d % 2], nc.vector)

from contextlib import ExitStack

import concourse.mybir as mybir
from concourse.masks import make_identity

F32 = mybir.dt.float32
BF16 = mybir.dt.bfloat16
U32 = mybir.dt.uint32
U8 = mybir.dt.uint8
FP8X4 = mybir.dt.float8_e4m3fn_x4
ALU = mybir.AluOpType
ACT = mybir.ActivationFunctionType
AX = mybir.AxisListType

P = 128
TOKENS = 4096
H = 1024
P0 = 512
V0 = 1024
TILES = TOKENS // P
PAIRS = TILES // 2

FLOPS = 2 * TOKENS * H * P0 + 2 * TOKENS * P0 * V0

MANUAL = 0
QUADS = 8
XC_V = 1
HC_VMOD = 4
B_FIRST = 2
RB = 4
DELAY = 2
TAIL = 6
W_AFTER = 4
W_STEP = 5
XBUFS = 5


def tile_adaptiveinputsoftmax_pa_t_kernel(tc, x, tail_proj_0, tail_w_0, cluster_prob, out):
    nc = tc.nc
    with ExitStack() as ctx:
        const = ctx.enter_context(tc.tile_pool(name="const", bufs=1))
        xg_pool = ctx.enter_context(tc.tile_pool(name="xg_pool", bufs=2))
        x_pool = ctx.enter_context(tc.tile_pool(name="x_pool", bufs=XBUFS))
        hg_pool = ctx.enter_context(tc.tile_pool(name="hg_pool", bufs=3))
        e_pool = ctx.enter_context(tc.tile_pool(name="e_pool", bufs=5))
        st_pool = ctx.enter_context(tc.tile_pool(name="st_pool", bufs=8))
        ps_pool = ctx.enter_context(tc.psum_pool(name="ps_pool", bufs=1))
        if MANUAL:
            ctx.enter_context(tc.manual_schedule())

        x_rows = x.flatten_outer_dims().rearrange("(p i) k -> p (i k)", i=TILES)
        out_rows = out.flatten_outer_dims().rearrange("(p i) v -> p (i v)", i=TILES)
        prob_rows = cluster_prob.rearrange("n t o -> (n t o)").rearrange("(p i) -> p i", i=TILES)

        ident = const.tile([P, P], F32, name="ident")
        make_identity(nc, ident[:])
        warm_in = const.tile([P, 1], F32, name="warm_in")
        warm_out = const.tile([P, 1], F32, name="warm_out")
        nc.vector.memset(warm_in[:], 0.0)
        nc.scalar.activation(out=warm_out[:], in_=warm_in[:], func=ACT.Exp)

        p_raw = const.tile([P, 4096], BF16, name="p_raw")
        p_grp = const.tile([P, 4096], BF16, name="p_grp", align_bytes=64)
        p_cod = const.tile([P, 1024], U32, name="p_cod", align_bytes=64)
        p_scl = const.tile([P, 1024], U8, name="p_scl", align_bytes=64)
        w_raw = const.tile([P, 4096], BF16, name="w_raw")
        w_grp = const.tile([P, 4096], BF16, name="w_grp", align_bytes=64)
        w_cod = const.tile([P, 1024], U32, name="w_cod", align_bytes=64)
        w_scl = const.tile([P, 1024], U8, name="w_scl", align_bytes=64)
        prob_bf = const.tile([P, TILES], BF16, name="prob_bf")
        prob = const.tile([P, TILES], F32, name="prob")
        h_cod = const.tile([P, TOKENS], U32, name="h_cod", align_bytes=64)
        h_scl = const.tile([P, TOKENS], U8, name="h_scl", align_bytes=64)
        x_cod = const.tile([P, 2 * TOKENS], U32, name="x_cod", align_bytes=64)
        x_scl = const.tile([P, 2 * TOKENS], U8, name="x_scl", align_bytes=64)
        x_sb = []
        for g in range(8):
            xs = x_pool.tile([P, 4096], BF16, name="xs")
            x_sb.append(xs)

        for c in range(2):
            nc.sync.dma_start(
                out=p_raw[:, 2048 * c : 2048 * (c + 1)].rearrange("p (u m) -> p u m", u=2),
                in_=tail_proj_0[512 * c : 512 * (c + 1), :].rearrange("(u p e) n -> p u (e n)", u=2, e=2),
            )
        for a in range(2):
            nc.sync.dma_start(out=x_sb[0][:, 2048 * a : 2048 * (a + 1)], in_=x_rows[:, 2048 * a : 2048 * (a + 1)])
        for g in range(1, 8):
            nc.sync.dma_start(out=x_sb[g][:], in_=x_rows[:, 4096 * g : 4096 * (g + 1)])
            if g == W_AFTER:
                nc.sync.dma_start(
                    out=w_raw[:].rearrange("p (t n) -> p t n", t=4),
                    in_=tail_w_0.rearrange("(t p) n -> p t n", t=4),
                )
                nc.sync.dma_start(out=prob_bf[:], in_=prob_rows)

        def prepare_proj():
            for c in range(2):
                cols = slice(2048 * c, 2048 * (c + 1))
                nc.vector.tensor_copy(
                    out=p_grp[:, cols].rearrange("p (a i t) -> p a t i", i=4, t=4),
                    in_=p_raw[:, cols].rearrange("p (t a i) -> p a t i", t=4, i=4),
                )
            for c in range(2):
                nc.vector.quantize_mx(
                    out=p_cod[:, 512 * c : 512 * (c + 1)].bitcast(FP8X4),
                    scales=p_scl[:, 512 * c : 512 * (c + 1)],
                    in_=p_grp[:, 2048 * c : 2048 * (c + 1)],
                )

        def prepare_w():
            planes = w_raw[:].rearrange("p (t n) -> p t n", t=4)
            for v in range(2):
                nc.vector.tensor_copy(
                    out=w_grp[:, 2048 * v : 2048 * (v + 1)].rearrange("p (a i t) -> p a t i", i=4, t=4),
                    in_=planes[:, :, 512 * v : 512 * (v + 1)].rearrange("p t (a i) -> p a t i", i=4),
                )
            for v in range(2):
                nc.vector.quantize_mx(
                    out=w_cod[:, 512 * v : 512 * (v + 1)].bitcast(FP8X4),
                    scales=w_scl[:, 512 * v : 512 * (v + 1)],
                    in_=w_grp[:, 2048 * v : 2048 * (v + 1)],
                )
            nc.vector.tensor_copy(out=prob[:], in_=prob_bf[:])

        xt_of = {}
        xg_of = {}
        ht_of = {}
        hg_of = {}
        lg_of = {}
        mx_of = {}
        e_of = {}
        sm_of = {}
        rc_of = {}

        def bank(b, name):
            return ps_pool.tile([P, 512], F32, name=name, offset=2048 * b)

        def transposes(g):
            words = x_sb[g][:].bitcast(F32)
            for j in range(4):
                xt = bank(j, "xt")
                for s in range(4):
                    first = 512 * j + P * s
                    nc.tensor.transpose(xt[:, P * s : P * (s + 1)], words[:, first : first + P], ident[:])
                xt_of[4 * g + j] = xt

        def copy_x(g):
            xg = xg_pool.tile([P, 4096], BF16, name="xg", align_bytes=64)
            xg_of[g] = xg
            for j in range(4):
                copy = nc.vector.tensor_copy if j >= 4 - XC_V else nc.scalar.copy
                copy(
                    out=xg[:, 1024 * j : 1024 * (j + 1)].bitcast(F32).rearrange("p (c r u) -> p c r u", c=2, u=2),
                    in_=xt_of[4 * g + j][:].rearrange("p (c u r) -> p c r u", c=2, u=2),
                )

        def quantise_x(g):
            for a in range(2):
                cols = slice(1024 * g + 512 * a, 1024 * g + 512 * (a + 1))
                nc.vector.quantize_mx(
                    out=x_cod[:, cols].bitcast(FP8X4), scales=x_scl[:, cols], in_=xg_of[g][:, 2048 * a : 2048 * (a + 1)]
                )

        def stage1(i):
            ht = bank(4 + i % 4, "ht")
            ht_of[i] = ht
            for t in range(4):
                for c in range(2):
                    wcols = slice(512 * c + P * t, 512 * c + P * (t + 1))
                    xcols = slice(256 * i + P * c, 256 * i + P * (c + 1))
                    nc.tensor.matmul_mx(
                        out=ht[:, P * t : P * (t + 1)],
                        lhsT=p_cod[:, wcols].bitcast(FP8X4),
                        lhsT_scale=p_scl[:, wcols],
                        rhs=x_cod[:, xcols].bitcast(FP8X4),
                        rhs_scale=x_scl[:, xcols],
                        start=(c == 0),
                        stop=(c == 1),
                    )

        def copy_h(i):
            q, a = divmod(i, 2)
            if a == 0:
                hg = hg_pool.tile([P, 1024], BF16, name="hg", align_bytes=64)
                hg_of[q] = hg
            copy = nc.vector.tensor_copy if i % HC_VMOD == HC_VMOD - 1 else nc.scalar.copy
            copy(
                out=hg_of[q][:, 512 * a : 512 * (a + 1)].rearrange("p (r t) -> p r t", t=4),
                in_=ht_of[i][:].rearrange("p (t r) -> p r t", t=4),
            )
            if a == 1:
                cols = slice(256 * q, 256 * (q + 1))
                nc.vector.quantize_mx(out=h_cod[:, cols].bitcast(FP8X4), scales=h_scl[:, cols], in_=hg_of[q][:])

        def stage2(i, banks):
            for v in range(2):
                lg = bank(banks[v], "lg")
                nc.tensor.matmul_mx(
                    out=lg[:],
                    lhsT=h_cod[:, P * i : P * (i + 1)].bitcast(FP8X4),
                    lhsT_scale=h_scl[:, P * i : P * (i + 1)],
                    rhs=w_cod[:, 512 * v : 512 * (v + 1)].bitcast(FP8X4),
                    rhs_scale=w_scl[:, 512 * v : 512 * (v + 1)],
                    start=True,
                    stop=True,
                )
                lg_of[(i, v)] = lg

        def row_max(i):
            mx = st_pool.tile([P, 4], F32, name="mx")
            mx_of[i] = mx
            for v in range(2):
                nc.vector.tensor_reduce(out=mx[:, v : v + 1], in_=lg_of[(i, v)][:], axis=AX.X, op=ALU.max)
            nc.vector.tensor_reduce(out=mx[:, 2:3], in_=mx[:, 0:2], axis=AX.X, op=ALU.max, negate=True)

        def exponent(i):
            q, a = divmod(i, 2)
            if a == 0:
                e = e_pool.tile([P, 2048], F32, name="e")
                sm = st_pool.tile([P, 4], F32, name="sm")
                rc = st_pool.tile([P, 4], F32, name="rc")
                e_of[q] = e
                sm_of[q] = sm
                rc_of[q] = rc
            for v in range(2):
                first = 1024 * a + 512 * v
                nc.scalar.activation(
                    out=e_of[q][:, first : first + 512],
                    in_=lg_of[(i, v)][:],
                    func=ACT.Exp,
                    bias=mx_of[i][:, 2:3],
                    scale=1.0,
                    accum_out=sm_of[q][:, 2 * a + v : 2 * a + v + 1],
                )

        def finish(q, halves, engine):
            lo, n = halves[0], len(halves)
            sm = sm_of[q]
            rc = rc_of[q]
            nc.vector.tensor_reduce(
                out=rc[:, lo : lo + n],
                in_=sm[:, 2 * lo : 2 * (lo + n)].rearrange("p (a v) -> p a v", v=2),
                axis=AX.X,
                op=ALU.add,
            )
            nc.vector.reciprocal(out=rc[:, 2 + lo : 2 + lo + n], in_=rc[:, lo : lo + n])
            for a in halves:
                i = 2 * q + a
                part = e_of[q][:, 1024 * a : 1024 * (a + 1)]
                engine.tensor_scalar(
                    out=part,
                    in0=part,
                    scalar1=rc[:, 2 + a : 3 + a],
                    scalar2=prob[:, i : i + 1],
                    op0=ALU.mult,
                    op1=ALU.mult,
                )
                nc.sync.dma_start(out=out_rows[:, 1024 * i : 1024 * (i + 1)], in_=part)

        state = {"b": 0, "c": 0}

        def front_tile():
            i = state["b"]
            stage1(i)
            copy_h(i)
            state["b"] = i + 1

        def soft_tile(banks):
            i = state["c"]
            stage2(i, banks)
            row_max(i)
            exponent(i)
            state["c"] = i + 1
            d = i - DELAY
            if d >= 0 and d % 2 == 1 and d < TILES - TAIL:
                finish(d // 2, [0, 1], nc.gpsimd)

        prepare_proj()
        for g in range(QUADS):
            transposes(g)
            copy_x(g)
            if g >= B_FIRST:
                front_tile()
            quantise_x(g)
            if g == W_STEP:
                prepare_w()
        while state["b"] < TILES:
            for k in range(RB):
                if state["b"] < TILES:
                    front_tile()
            c = state["c"]
            soft_tile([(2 * c) % 4, (2 * c + 1) % 4])
        if state["c"] % 2 == 1:
            c = state["c"]
            soft_tile([(2 * c) % 4, (2 * c + 1) % 4])
        c0 = state["c"]
        while state["c"] < TILES:
            c = state["c"]
            soft_tile([(2 * (c - c0) + 4) % 8, (2 * (c - c0) + 5) % 8])
        for d in range(TILES - DELAY, TILES):
            if d % 2 == 1 and d < TILES - TAIL:
                finish(d // 2, [0, 1], nc.gpsimd)
        for d in range(TILES - TAIL, TILES):
            finish(d // 2, [d % 2], nc.vector)
